import numpy as np
import ml_dtypes


def mxq(x, axis, fmt="e4m3"):
    dtype, down = {"e4m3": (ml_dtypes.float8_e4m3fn, 7), "e5m2": (ml_dtypes.float8_e5m2, 14)}[fmt]
    v = np.moveaxis(np.asarray(x, np.float32).astype(ml_dtypes.bfloat16).astype(np.float64), axis, -1)
    blocks = v.reshape(v.shape[:-1] + (-1, 32))
    amax = np.abs(blocks).max(-1, keepdims=True)
    byte = np.maximum(np.where(amax > 0, np.frexp(amax)[1] - 1 + 127, 0) - down, 1)
    scale = np.exp2(byte - 127.0)
    codes = (blocks / scale).astype(np.float32).astype(dtype).astype(np.float64)
    return np.moveaxis((codes * scale).reshape(v.shape), -1, axis)


WIDE = False


def mx_kscale(k):
    if not WIDE:
        return np.ones(k)
    levels = np.array([10, -10, 5, -5, 0])
    a = np.random.permutation(np.resize(levels, k // 512 * 4)).reshape(k // 512, 4)
    idx = np.arange(k)
    return np.exp2(a[idx // 512, idx % 128 // 32])


BF16 = ml_dtypes.bfloat16


def bf(x):
    return np.asarray(x, np.float32).astype(BF16)


def f64(x):
    return np.asarray(x).astype(np.float64)


B, IN, MEM, CTX, H, G = 4096, 512, 512, 1024, 4, 3


def sigmoid(v):
    return 1.0 / (1.0 + np.exp(-v))


def setup_inputs():
    s = mx_kscale(IN)
    w = np.random.standard_normal((MEM, MEM + IN)) / np.sqrt(MEM + IN)
    w[:, MEM:] = w[:, MEM:] / s
    return {"input_tensor": bf(np.random.standard_normal((B, IN)) * s),
            "previous_memory": bf(np.random.standard_normal((B, MEM))),
            "fg_w": bf(w),
            "fg_b": bf(np.random.standard_normal(MEM) * 0.3)}


def reference(input_tensor, previous_memory, fg_w, fg_b):
    m = f64(previous_memory)
    forget_in = np.concatenate([m, f64(input_tensor)], axis=-1)
    fgate = sigmoid((mxq(forget_in, 1, "e4m3") @ mxq(f64(fg_w), 1, "e4m3").T) + f64(fg_b))
    return m * fgate

@@ -1,0 +1,177 @@
+from contextlib import ExitStack
+
+import concourse.mybir as mybir
+from concourse.masks import make_identity
+
+F32 = mybir.dt.float32
+BF16 = mybir.dt.bfloat16
+U32 = mybir.dt.uint32
+U8 = mybir.dt.uint8
+FP8X4 = mybir.dt.float8_e4m3fn_x4
+ADD = mybir.AluOpType.add
+MULT = mybir.AluOpType.mult
+SIGMOID = mybir.ActivationFunctionType.Sigmoid
+
+P = 128
+BATCH = 4096
+FEAT = 512
+PASSES = 2
+PACK = 4
+WORDS = FEAT // 2
+HALVES = WORDS // P
+ROWS_PER_PARTITION = BATCH // P
+CHUNK = 4
+CHUNKS = ROWS_PER_PARTITION // CHUNK
+QUANT = 2
+GPSIMD_TILES = 2
+W_TILES = FEAT // P
+
+FLOPS = 2 * BATCH * (PASSES * FEAT) * FEAT
+
+
+def tile_dynamicmemorycell_pa_t_kernel(tc, input_tensor, previous_memory, fg_w, fg_b, out):
+    nc = tc.nc
+
+    m_rows = previous_memory.rearrange("(p r) k -> p r k", r=ROWS_PER_PARTITION)
+    x_rows = input_tensor.rearrange("(p r) k -> p r k", r=ROWS_PER_PARTITION)
+    out_rows = out.rearrange("(p r) n -> p r n", r=ROWS_PER_PARTITION)
+
+    with ExitStack() as ctx:
+        consts = ctx.enter_context(tc.tile_pool(name="consts", bufs=1))
+        inputs = ctx.enter_context(tc.tile_pool(name="inputs", bufs=CHUNKS))
+        stage = ctx.enter_context(tc.tile_pool(name="stage", bufs=3))
+        results = ctx.enter_context(tc.tile_pool(name="results", bufs=4))
+        psum_t = ctx.enter_context(tc.psum_pool(name="psum_t", bufs=4))
+        psum_acc = ctx.enter_context(tc.psum_pool(name="psum_acc", bufs=4))
+        ctx.enter_context(tc.manual_schedule())
+
+        w_sb = consts.tile([P, W_TILES, PASSES * FEAT], BF16)
+        for j in range(W_TILES):
+            nc.sync.dma_start(out=w_sb[:, j, :], in_=fg_w[j * P : (j + 1) * P, :])
+        bias = consts.tile([P, FEAT], BF16)
+        nc.scalar.dma_start(out=bias[:], in_=fg_b.partition_broadcast(P))
+        m_chunks = []
+        x_chunks = []
+        for c in range(CHUNKS):
+            rows = slice(c * CHUNK, (c + 1) * CHUNK)
+            m_sb = inputs.tile([P, CHUNK, FEAT], BF16)
+            nc.sync.dma_start(out=m_sb[:], in_=m_rows[:, rows, :])
+            x_sb = inputs.tile([P, CHUNK, FEAT], BF16)
+            nc.sync.dma_start(out=x_sb[:], in_=x_rows[:, rows, :])
+            m_chunks.append(m_sb)
+            x_chunks.append(x_sb)
+
+        ident = consts.tile([P, P], F32)
+        make_identity(nc, ident[:])
+        warm = consts.tile([P, 1], F32)
+        nc.vector.memset(warm[:], 0.0)
+        nc.scalar.activation(out=warm[:], in_=warm[:], func=SIGMOID)
+
+        w_words = w_sb[:].bitcast(F32)
+        w_grouped = consts.tile([P, PASSES, FEAT, PACK], BF16, align_bytes=64)
+        w_grouped_words = w_grouped[:].bitcast(F32)
+        for j in range(W_TILES):
+            wt = psum_t.tile([P, PASSES * HALVES, P], F32, tag="xt")
+            for q in range(PASSES * HALVES):
+                nc.tensor.transpose(wt[:, q, :], w_words[:, j, q * P : (q + 1) * P], ident[:])
+            nc.vector.tensor_copy(
+                out=w_grouped_words[:, :, j * P : (j + 1) * P, :],
+                in_=wt[:].rearrange("p (g u) n -> p g n u", u=HALVES),
+            )
+        w_codes = consts.tile([P, PASSES, FEAT], U32, align_bytes=64)
+        w_scales = consts.tile([P, PASSES, FEAT], U8, align_bytes=64)
+        for g in range(PASSES):
+            nc.vector.quantize_mx(
+                out=w_codes[:, g, :].bitcast(FP8X4),
+                scales=w_scales[:, g, :],
+                in_=w_grouped[:, g, :, :].rearrange("p n t -> p (n t)"),
+            )
+
+        banks = {}
+        grouped_of = {}
+        codes_of = {}
+        scales_of = {}
+        acc_of = {}
+        z_of = {}
+
+        def transposes(c):
+            for r in range(CHUNK):
+                xt = psum_t.tile([P, PASSES * HALVES, P], F32, tag="xt")
+                for g, src in enumerate((m_chunks[c], x_chunks[c])):
+                    words = src[:].bitcast(F32)
+                    for u in range(HALVES):
+                        nc.tensor.transpose(
+                            xt[:, g * HALVES + u, :], words[:, r, u * P : (u + 1) * P], ident[:]
+                        )
+                banks[(c, r)] = xt
+
+        def regroup(c):
+            grouped = stage.tile([P, CHUNK, PASSES, P, PACK], BF16, align_bytes=64)
+            grouped_words = grouped[:].bitcast(F32)
+            for r in range(CHUNK):
+                nc.scalar.copy(
+                    out=grouped_words[:, r, :, :, :],
+                    in_=banks[(c, r)][:].rearrange("p (g u) b -> p g b u", u=HALVES),
+                )
+            grouped_of[c] = grouped
+
+        def quantise(c):
+            codes = stage.tile([P, CHUNK, PASSES, P], U32, align_bytes=64)
+            scales = stage.tile([P, CHUNK, PASSES, P], U8, align_bytes=64)
+            for r in range(0, CHUNK, QUANT):
+                nc.vector.quantize_mx(
+                    out=codes[:, r : r + QUANT, :, :].rearrange("p r g b -> p (r g b)").bitcast(FP8X4),
+                    scales=scales[:, r : r + QUANT, :, :].rearrange("p r g b -> p (r g b)"),
+                    in_=grouped_of[c][:, r : r + QUANT, :, :, :].rearrange("p r g b t -> p (r g b t)"),
+                )
+            codes_of[c] = codes
+            scales_of[c] = scales
+
+        def matmuls(c):
+            for r in range(CHUNK):
+                acc = psum_acc.tile([P, FEAT], F32)
+                for g in range(PASSES):
+                    nc.tensor.matmul_mx(
+                        out=acc[:],
+                        lhsT=codes_of[c][:, r, g, :].bitcast(FP8X4),
+                        lhsT_scale=scales_of[c][:, r, g, :],
+                        rhs=w_codes[:, g, :].bitcast(FP8X4),
+                        rhs_scale=w_scales[:, g, :],
+                        start=(g == 0),
+                        stop=(g == PASSES - 1),
+                    )
+                acc_of[(c, r)] = acc
+
+        def add_bias(c):
+            z = results.tile([P, CHUNK, FEAT], F32)
+            for r in range(CHUNK):
+                nc.vector.tensor_tensor(out=z[:, r, :], in0=acc_of[(c, r)][:], in1=bias[:], op=ADD)
+            z_of[c] = z
+
+        def gate(c):
+            for r in range(CHUNK):
+                nc.scalar.activation(out=z_of[c][:, r, :], in_=z_of[c][:, r, :], func=SIGMOID)
+
+        def multiply_and_store(c):
+            z = z_of[c]
+            for r in range(GPSIMD_TILES):
+                nc.gpsimd.tensor_tensor(out=z[:, r, :], in0=z[:, r, :], in1=m_chunks[c][:, r, :], op=MULT)
+            nc.vector.tensor_tensor(
+                out=z[:, GPSIMD_TILES:, :], in0=z[:, GPSIMD_TILES:, :], in1=m_chunks[c][:, GPSIMD_TILES:, :], op=MULT
+            )
+            nc.sync.dma_start(out=out_rows[:, c * CHUNK : (c + 1) * CHUNK, :], in_=z[:])
+
+        transposes(0)
+        regroup(0)
+        quantise(0)
+        for c in range(CHUNKS):
+            if c + 1 < CHUNKS:
+                transposes(c + 1)
+            matmuls(c)
+            if c + 1 < CHUNKS:
+                regroup(c + 1)
+            add_bias(c)
+            if c + 1 < CHUNKS:
+                quantise(c + 1)
+            gate(c)
+            multiply_and_store(c)

@@ -23,7 +23,6 @@ ROWS_PER_PARTITION = BATCH // P
 CHUNK = 4
 CHUNKS = ROWS_PER_PARTITION // CHUNK
 QUANT = 2
-GPSIMD_TILES = 2
 W_TILES = FEAT // P
 
 FLOPS = 2 * BATCH * (PASSES * FEAT) * FEAT
@@ -154,11 +153,7 @@ def tile_dynamicmemorycell_pa_t_kernel(tc, input_tensor, previous_memory, fg_w, 
 
         def multiply_and_store(c):
             z = z_of[c]
-            for r in range(GPSIMD_TILES):
-                nc.gpsimd.tensor_tensor(out=z[:, r, :], in0=z[:, r, :], in1=m_chunks[c][:, r, :], op=MULT)
-            nc.vector.tensor_tensor(
-                out=z[:, GPSIMD_TILES:, :], in0=z[:, GPSIMD_TILES:, :], in1=m_chunks[c][:, GPSIMD_TILES:, :], op=MULT
-            )
+            nc.vector.tensor_tensor(out=z[:], in0=z[:], in1=m_chunks[c][:], op=MULT)
             nc.sync.dma_start(out=out_rows[:, c * CHUNK : (c + 1) * CHUNK, :], in_=z[:])
 
         transposes(0)

@@ -8,7 +8,6 @@ BF16 = mybir.dt.bfloat16
 U32 = mybir.dt.uint32
 U8 = mybir.dt.uint8
 FP8X4 = mybir.dt.float8_e4m3fn_x4
-ADD = mybir.AluOpType.add
 MULT = mybir.AluOpType.mult
 SIGMOID = mybir.ActivationFunctionType.Sigmoid
 
@@ -17,13 +16,12 @@ BATCH = 4096
 FEAT = 512
 PASSES = 2
 PACK = 4
-WORDS = FEAT // 2
-HALVES = WORDS // P
+HALVES = 2
+BLOCKS = PASSES * HALVES
 ROWS_PER_PARTITION = BATCH // P
 CHUNK = 4
 CHUNKS = ROWS_PER_PARTITION // CHUNK
-QUANT = 2
-W_TILES = FEAT // P
+N_TILES = FEAT // P
 
 FLOPS = 2 * BATCH * (PASSES * FEAT) * FEAT
 
@@ -39,16 +37,14 @@ def tile_dynamicmemorycell_pa_t_kernel(tc, input_tensor, previous_memory, fg_w, 
         consts = ctx.enter_context(tc.tile_pool(name="consts", bufs=1))
         inputs = ctx.enter_context(tc.tile_pool(name="inputs", bufs=CHUNKS))
         stage = ctx.enter_context(tc.tile_pool(name="stage", bufs=3))
-        results = ctx.enter_context(tc.tile_pool(name="results", bufs=4))
-        psum_t = ctx.enter_context(tc.psum_pool(name="psum_t", bufs=4))
-        psum_acc = ctx.enter_context(tc.psum_pool(name="psum_acc", bufs=4))
+        psum_t = ctx.enter_context(tc.psum_pool(name="psum_t", bufs=2))
+        psum_z = ctx.enter_context(tc.psum_pool(name="psum_z", bufs=N_TILES))
+        psum_o = ctx.enter_context(tc.psum_pool(name="psum_o", bufs=2))
         ctx.enter_context(tc.manual_schedule())
 
-        w_sb = consts.tile([P, W_TILES, PASSES * FEAT], BF16)
-        for j in range(W_TILES):
+        w_sb = consts.tile([P, N_TILES, PASSES * FEAT], BF16)
+        for j in range(N_TILES):
             nc.sync.dma_start(out=w_sb[:, j, :], in_=fg_w[j * P : (j + 1) * P, :])
-        bias = consts.tile([P, FEAT], BF16)
-        nc.scalar.dma_start(out=bias[:], in_=fg_b.partition_broadcast(P))
         m_chunks = []
         x_chunks = []
         for c in range(CHUNKS):
@@ -66,12 +62,22 @@ def tile_dynamicmemorycell_pa_t_kernel(tc, input_tensor, previous_memory, fg_w, 
         nc.vector.memset(warm[:], 0.0)
         nc.scalar.activation(out=warm[:], in_=warm[:], func=SIGMOID)
 
+        bias_rows = consts.tile([P, P], BF16)
+        nc.vector.memset(bias_rows[:], 0.0)
+        nc.scalar.dma_start(out=bias_rows[0:N_TILES, :], in_=fg_b.rearrange("(j n) -> j n", n=P))
+        bias_rows_f32 = consts.tile([P, P], F32)
+        nc.vector.tensor_copy(out=bias_rows_f32[:], in_=bias_rows[:])
+        bias_t = psum_t.tile([P, BLOCKS, P], F32, tag="xt")
+        nc.tensor.transpose(bias_t[:, 0, :], bias_rows_f32[:], ident[:])
+        bias_col = consts.tile([P, N_TILES], F32)
+        nc.vector.tensor_copy(out=bias_col[:], in_=bias_t[:, 0, 0:N_TILES])
+
         w_words = w_sb[:].bitcast(F32)
         w_grouped = consts.tile([P, PASSES, FEAT, PACK], BF16, align_bytes=64)
         w_grouped_words = w_grouped[:].bitcast(F32)
-        for j in range(W_TILES):
-            wt = psum_t.tile([P, PASSES * HALVES, P], F32, tag="xt")
-            for q in range(PASSES * HALVES):
+        for j in range(N_TILES):
+            wt = psum_t.tile([P, BLOCKS, P], F32, tag="xt")
+            for q in range(BLOCKS):
                 nc.tensor.transpose(wt[:, q, :], w_words[:, j, q * P : (q + 1) * P], ident[:])
             nc.vector.tensor_copy(
                 out=w_grouped_words[:, :, j * P : (j + 1) * P, :],
@@ -86,87 +92,78 @@ def tile_dynamicmemorycell_pa_t_kernel(tc, input_tensor, previous_memory, fg_w, 
                 in_=w_grouped[:, g, :, :].rearrange("p n t -> p (n t)"),
             )
 
-        banks = {}
         grouped_of = {}
         codes_of = {}
         scales_of = {}
-        acc_of = {}
-        z_of = {}
+        gate_of = {}
+        result_of = {}
 
-        def transposes(c):
-            for r in range(CHUNK):
-                xt = psum_t.tile([P, PASSES * HALVES, P], F32, tag="xt")
-                for g, src in enumerate((m_chunks[c], x_chunks[c])):
-                    words = src[:].bitcast(F32)
-                    for u in range(HALVES):
-                        nc.tensor.transpose(
-                            xt[:, g * HALVES + u, :], words[:, r, u * P : (u + 1) * P], ident[:]
-                        )
-                banks[(c, r)] = xt
-
-        def regroup(c):
-            grouped = stage.tile([P, CHUNK, PASSES, P, PACK], BF16, align_bytes=64)
-            grouped_words = grouped[:].bitcast(F32)
-            for r in range(CHUNK):
-                nc.scalar.copy(
-                    out=grouped_words[:, r, :, :, :],
-                    in_=banks[(c, r)][:].rearrange("p (g u) b -> p g b u", u=HALVES),
-                )
-            grouped_of[c] = grouped
+        def transpose_inputs(c, r):
+            if r == 0:
+                grouped = stage.tile([P, PASSES, CHUNK, P, PACK], BF16, align_bytes=64)
+                grouped_of[c] = grouped
+            xt = psum_t.tile([P, BLOCKS, P], F32, tag="xt")
+            for g, src in enumerate((m_chunks[c], x_chunks[c])):
+                words = src[:].bitcast(F32)
+                for u in range(HALVES):
+                    nc.tensor.transpose(xt[:, g * HALVES + u, :], words[:, r, u * P : (u + 1) * P], ident[:])
+            copy = nc.vector.tensor_copy if r == 0 else nc.scalar.copy
+            copy(
+                out=grouped_of[c][:].bitcast(F32)[:, :, r, :, :],
+                in_=xt[:].rearrange("p (g u) b -> p g b u", u=HALVES),
+            )
 
         def quantise(c):
-            codes = stage.tile([P, CHUNK, PASSES, P], U32, align_bytes=64)
-            scales = stage.tile([P, CHUNK, PASSES, P], U8, align_bytes=64)
-            for r in range(0, CHUNK, QUANT):
+            codes = stage.tile([P, PASSES, CHUNK * P], U32, align_bytes=64)
+            scales = stage.tile([P, PASSES, CHUNK * P], U8, align_bytes=64)
+            for g in range(PASSES):
                 nc.vector.quantize_mx(
-                    out=codes[:, r : r + QUANT, :, :].rearrange("p r g b -> p (r g b)").bitcast(FP8X4),
-                    scales=scales[:, r : r + QUANT, :, :].rearrange("p r g b -> p (r g b)"),
-                    in_=grouped_of[c][:, r : r + QUANT, :, :, :].rearrange("p r g b t -> p (r g b t)"),
+                    out=codes[:, g, :].bitcast(FP8X4),
+                    scales=scales[:, g, :],
+                    in_=grouped_of[c][:, g, :, :, :].rearrange("p r b t -> p (r b t)"),
                 )
             codes_of[c] = codes
             scales_of[c] = scales
 
-        def matmuls(c):
-            for r in range(CHUNK):
-                acc = psum_acc.tile([P, FEAT], F32)
+        def matmuls_and_gate(c):
+            gate = stage.tile([P, N_TILES, CHUNK * P], F32)
+            for j in range(N_TILES):
+                features = slice(j * P, (j + 1) * P)
+                sums = psum_z.tile([P, CHUNK * P], F32)
                 for g in range(PASSES):
                     nc.tensor.matmul_mx(
-                        out=acc[:],
-                        lhsT=codes_of[c][:, r, g, :].bitcast(FP8X4),
-                        lhsT_scale=scales_of[c][:, r, g, :],
-                        rhs=w_codes[:, g, :].bitcast(FP8X4),
-                        rhs_scale=w_scales[:, g, :],
+                        out=sums[:],
+                        lhsT=w_codes[:, g, features].bitcast(FP8X4),
+                        lhsT_scale=w_scales[:, g, features],
+                        rhs=codes_of[c][:, g, :].bitcast(FP8X4),
+                        rhs_scale=scales_of[c][:, g, :],
                         start=(g == 0),
                         stop=(g == PASSES - 1),
                     )
-                acc_of[(c, r)] = acc
+                nc.scalar.activation(out=gate[:, j, :], in_=sums[:], func=SIGMOID, bias=bias_col[:, j : j + 1])
+            gate_of[c] = gate
 
-        def add_bias(c):
-            z = results.tile([P, CHUNK, FEAT], F32)
-            for r in range(CHUNK):
-                nc.vector.tensor_tensor(out=z[:, r, :], in0=acc_of[(c, r)][:], in1=bias[:], op=ADD)
-            z_of[c] = z
+        def transpose_gate_and_multiply(c, r):
+            if r == 0:
+                result = stage.tile([P, CHUNK, FEAT], F32)
+                result_of[c] = result
+            gate_t = psum_o.tile([P, FEAT], F32)
+            for j in range(N_TILES):
+                nc.tensor.transpose(gate_t[:, j * P : (j + 1) * P], gate_of[c][:, j, r * P : (r + 1) * P], ident[:])
+            nc.vector.tensor_tensor(out=result_of[c][:, r, :], in0=gate_t[:], in1=m_chunks[c][:, r, :], op=MULT)
 
-        def gate(c):
-            for r in range(CHUNK):
-                nc.scalar.activation(out=z_of[c][:, r, :], in_=z_of[c][:, r, :], func=SIGMOID)
-
-        def multiply_and_store(c):
-            z = z_of[c]
-            nc.vector.tensor_tensor(out=z[:], in0=z[:], in1=m_chunks[c][:], op=MULT)
-            nc.sync.dma_start(out=out_rows[:, c * CHUNK : (c + 1) * CHUNK, :], in_=z[:])
-
-        transposes(0)
-        regroup(0)
+        for r in range(CHUNK):
+            transpose_inputs(0, r)
         quantise(0)
-        for c in range(CHUNKS):
-            if c + 1 < CHUNKS:
-                transposes(c + 1)
-            matmuls(c)
-            if c + 1 < CHUNKS:
-                regroup(c + 1)
-            add_bias(c)
+        for c in range(CHUNKS + 1):
+            for step in range(CHUNK + 1):
+                if c + 1 < CHUNKS and step < CHUNK:
+                    transpose_inputs(c + 1, step)
+                if c >= 1 and step >= 1:
+                    transpose_gate_and_multiply(c - 1, step - 1)
+            if c >= 1:
+                nc.sync.dma_start(out=out_rows[:, (c - 1) * CHUNK : c * CHUNK, :], in_=result_of[c - 1][:])
             if c + 1 < CHUNKS:
                 quantise(c + 1)
-            gate(c)
-            multiply_and_store(c)
+            if c < CHUNKS:
+                matmuls_and_gate(c)

@@ -8,6 +8,7 @@ BF16 = mybir.dt.bfloat16
 U32 = mybir.dt.uint32
 U8 = mybir.dt.uint8
 FP8X4 = mybir.dt.float8_e4m3fn_x4
+ADD = mybir.AluOpType.add
 MULT = mybir.AluOpType.mult
 SIGMOID = mybir.ActivationFunctionType.Sigmoid
 
@@ -19,8 +20,9 @@ PACK = 4
 HALVES = 2
 BLOCKS = PASSES * HALVES
 ROWS_PER_PARTITION = BATCH // P
-CHUNK = 4
-CHUNKS = ROWS_PER_PARTITION // CHUNK
+GROUP = 2
+GROUPS = ROWS_PER_PARTITION // GROUP
+LEAD = 2
 N_TILES = FEAT // P
 
 FLOPS = 2 * BATCH * (PASSES * FEAT) * FEAT
@@ -35,42 +37,36 @@ def tile_dynamicmemorycell_pa_t_kernel(tc, input_tensor, previous_memory, fg_w, 
 
     with ExitStack() as ctx:
         consts = ctx.enter_context(tc.tile_pool(name="consts", bufs=1))
-        inputs = ctx.enter_context(tc.tile_pool(name="inputs", bufs=CHUNKS))
-        stage = ctx.enter_context(tc.tile_pool(name="stage", bufs=3))
-        psum_t = ctx.enter_context(tc.psum_pool(name="psum_t", bufs=2))
-        psum_z = ctx.enter_context(tc.psum_pool(name="psum_z", bufs=N_TILES))
-        psum_o = ctx.enter_context(tc.psum_pool(name="psum_o", bufs=2))
+        inputs = ctx.enter_context(tc.tile_pool(name="inputs", bufs=GROUPS))
+        stage = ctx.enter_context(tc.tile_pool(name="stage", bufs=LEAD + 2))
+        psum_t = ctx.enter_context(tc.psum_pool(name="psum_t", bufs=2 * GROUP))
+        psum_acc = ctx.enter_context(tc.psum_pool(name="psum_acc", bufs=2 * GROUP))
         ctx.enter_context(tc.manual_schedule())
 
         w_sb = consts.tile([P, N_TILES, PASSES * FEAT], BF16)
         for j in range(N_TILES):
             nc.sync.dma_start(out=w_sb[:, j, :], in_=fg_w[j * P : (j + 1) * P, :])
-        m_chunks = []
-        x_chunks = []
-        for c in range(CHUNKS):
-            rows = slice(c * CHUNK, (c + 1) * CHUNK)
-            m_sb = inputs.tile([P, CHUNK, FEAT], BF16)
+        bias_row = consts.tile([P, FEAT], BF16)
+        nc.vector.memset(bias_row[:], 0.0)
+        nc.sync.dma_start(out=bias_row[0:1, :], in_=fg_b.rearrange("(o n) -> o n", o=1))
+        m_groups = []
+        x_groups = []
+        for i in range(GROUPS):
+            rows = slice(i * GROUP, (i + 1) * GROUP)
+            m_sb = inputs.tile([P, GROUP, FEAT], BF16)
             nc.sync.dma_start(out=m_sb[:], in_=m_rows[:, rows, :])
-            x_sb = inputs.tile([P, CHUNK, FEAT], BF16)
+            x_sb = inputs.tile([P, GROUP, FEAT], BF16)
             nc.sync.dma_start(out=x_sb[:], in_=x_rows[:, rows, :])
-            m_chunks.append(m_sb)
-            x_chunks.append(x_sb)
+            m_groups.append(m_sb)
+            x_groups.append(x_sb)
 
         ident = consts.tile([P, P], F32)
         make_identity(nc, ident[:])
+        ones = consts.tile([P, P], BF16)
+        nc.vector.memset(ones[:], 1.0)
         warm = consts.tile([P, 1], F32)
         nc.vector.memset(warm[:], 0.0)
         nc.scalar.activation(out=warm[:], in_=warm[:], func=SIGMOID)
-
-        bias_rows = consts.tile([P, P], BF16)
-        nc.vector.memset(bias_rows[:], 0.0)
-        nc.scalar.dma_start(out=bias_rows[0:N_TILES, :], in_=fg_b.rearrange("(j n) -> j n", n=P))
-        bias_rows_f32 = consts.tile([P, P], F32)
-        nc.vector.tensor_copy(out=bias_rows_f32[:], in_=bias_rows[:])
-        bias_t = psum_t.tile([P, BLOCKS, P], F32, tag="xt")
-        nc.tensor.transpose(bias_t[:, 0, :], bias_rows_f32[:], ident[:])
-        bias_col = consts.tile([P, N_TILES], F32)
-        nc.vector.tensor_copy(out=bias_col[:], in_=bias_t[:, 0, 0:N_TILES])
 
         w_words = w_sb[:].bitcast(F32)
         w_grouped = consts.tile([P, PASSES, FEAT, PACK], BF16, align_bytes=64)
@@ -92,78 +88,92 @@ def tile_dynamicmemorycell_pa_t_kernel(tc, input_tensor, previous_memory, fg_w, 
                 in_=w_grouped[:, g, :, :].rearrange("p n t -> p (n t)"),
             )
 
+        bias_sum = psum_acc.tile([P, FEAT], F32, tag="acc")
+        nc.tensor.matmul(out=bias_sum[:], lhsT=ones[:], rhs=bias_row[:], start=True, stop=True)
+        bias = consts.tile([P, FEAT], F32)
+        nc.vector.tensor_copy(out=bias[:], in_=bias_sum[:])
+
+        banks = {}
         grouped_of = {}
         codes_of = {}
         scales_of = {}
-        gate_of = {}
-        result_of = {}
+        acc_of = {}
+        z_of = {}
 
-        def transpose_inputs(c, r):
-            if r == 0:
-                grouped = stage.tile([P, PASSES, CHUNK, P, PACK], BF16, align_bytes=64)
-                grouped_of[c] = grouped
-            xt = psum_t.tile([P, BLOCKS, P], F32, tag="xt")
-            for g, src in enumerate((m_chunks[c], x_chunks[c])):
-                words = src[:].bitcast(F32)
-                for u in range(HALVES):
-                    nc.tensor.transpose(xt[:, g * HALVES + u, :], words[:, r, u * P : (u + 1) * P], ident[:])
-            copy = nc.vector.tensor_copy if r == 0 else nc.scalar.copy
-            copy(
-                out=grouped_of[c][:].bitcast(F32)[:, :, r, :, :],
-                in_=xt[:].rearrange("p (g u) b -> p g b u", u=HALVES),
-            )
+        def transposes(i):
+            for r in range(GROUP):
+                xt = psum_t.tile([P, BLOCKS, P], F32, tag="xt")
+                for g, src in enumerate((m_groups[i], x_groups[i])):
+                    words = src[:].bitcast(F32)
+                    for u in range(HALVES):
+                        nc.tensor.transpose(xt[:, g * HALVES + u, :], words[:, r, u * P : (u + 1) * P], ident[:])
+                banks[(i, r)] = xt
 
-        def quantise(c):
-            codes = stage.tile([P, PASSES, CHUNK * P], U32, align_bytes=64)
-            scales = stage.tile([P, PASSES, CHUNK * P], U8, align_bytes=64)
-            for g in range(PASSES):
-                nc.vector.quantize_mx(
-                    out=codes[:, g, :].bitcast(FP8X4),
-                    scales=scales[:, g, :],
-                    in_=grouped_of[c][:, g, :, :, :].rearrange("p r b t -> p (r b t)"),
+        def regroup(i):
+            grouped = stage.tile([P, GROUP, PASSES, P, PACK], BF16, align_bytes=64)
+            grouped_words = grouped[:].bitcast(F32)
+            for r in range(GROUP):
+                nc.scalar.copy(
+                    out=grouped_words[:, r, :, :, :],
+                    in_=banks[(i, r)][:].rearrange("p (g u) b -> p g b u", u=HALVES),
                 )
-            codes_of[c] = codes
-            scales_of[c] = scales
+            grouped_of[i] = grouped
 
-        def matmuls_and_gate(c):
-            gate = stage.tile([P, N_TILES, CHUNK * P], F32)
-            for j in range(N_TILES):
-                features = slice(j * P, (j + 1) * P)
-                sums = psum_z.tile([P, CHUNK * P], F32)
+        def quantise(i):
+            codes = stage.tile([P, GROUP, PASSES, P], U32, align_bytes=64)
+            scales = stage.tile([P, GROUP, PASSES, P], U8, align_bytes=64)
+            nc.vector.quantize_mx(
+                out=codes[:].rearrange("p r g b -> p (r g b)").bitcast(FP8X4),
+                scales=scales[:].rearrange("p r g b -> p (r g b)"),
+                in_=grouped_of[i][:].rearrange("p r g b t -> p (r g b t)"),
+            )
+            codes_of[i] = codes
+            scales_of[i] = scales
+
+        def matmuls(i):
+            for r in range(GROUP):
+                acc = psum_acc.tile([P, FEAT], F32, tag="acc")
                 for g in range(PASSES):
                     nc.tensor.matmul_mx(
-                        out=sums[:],
-                        lhsT=w_codes[:, g, features].bitcast(FP8X4),
-                        lhsT_scale=w_scales[:, g, features],
-                        rhs=codes_of[c][:, g, :].bitcast(FP8X4),
-                        rhs_scale=scales_of[c][:, g, :],
+                        out=acc[:],
+                        lhsT=codes_of[i][:, r, g, :].bitcast(FP8X4),
+                        lhsT_scale=scales_of[i][:, r, g, :],
+                        rhs=w_codes[:, g, :].bitcast(FP8X4),
+                        rhs_scale=w_scales[:, g, :],
                         start=(g == 0),
                         stop=(g == PASSES - 1),
                     )
-                nc.scalar.activation(out=gate[:, j, :], in_=sums[:], func=SIGMOID, bias=bias_col[:, j : j + 1])
-            gate_of[c] = gate
+                acc_of[(i, r)] = acc
 
-        def transpose_gate_and_multiply(c, r):
-            if r == 0:
-                result = stage.tile([P, CHUNK, FEAT], F32)
-                result_of[c] = result
-            gate_t = psum_o.tile([P, FEAT], F32)
-            for j in range(N_TILES):
-                nc.tensor.transpose(gate_t[:, j * P : (j + 1) * P], gate_of[c][:, j, r * P : (r + 1) * P], ident[:])
-            nc.vector.tensor_tensor(out=result_of[c][:, r, :], in0=gate_t[:], in1=m_chunks[c][:, r, :], op=MULT)
+        def add_bias(i):
+            z = stage.tile([P, GROUP, FEAT], F32)
+            for r in range(GROUP):
+                nc.vector.tensor_tensor(out=z[:, r, :], in0=acc_of[(i, r)][:], in1=bias[:], op=ADD)
+            z_of[i] = z
 
-        for r in range(CHUNK):
-            transpose_inputs(0, r)
-        quantise(0)
-        for c in range(CHUNKS + 1):
-            for step in range(CHUNK + 1):
-                if c + 1 < CHUNKS and step < CHUNK:
-                    transpose_inputs(c + 1, step)
-                if c >= 1 and step >= 1:
-                    transpose_gate_and_multiply(c - 1, step - 1)
-            if c >= 1:
-                nc.sync.dma_start(out=out_rows[:, (c - 1) * CHUNK : c * CHUNK, :], in_=result_of[c - 1][:])
-            if c + 1 < CHUNKS:
-                quantise(c + 1)
-            if c < CHUNKS:
-                matmuls_and_gate(c)
+        def gate(i):
+            for r in range(GROUP):
+                nc.scalar.activation(out=z_of[i][:, r, :], in_=z_of[i][:, r, :], func=SIGMOID)
+
+        def multiply_and_store(i):
+            z = z_of[i]
+            nc.vector.tensor_tensor(out=z[:, 0, :], in0=z[:, 0, :], in1=m_groups[i][:, 0, :], op=MULT)
+            nc.gpsimd.tensor_tensor(out=z[:, 1, :], in0=z[:, 1, :], in1=m_groups[i][:, 1, :], op=MULT)
+            nc.sync.dma_start(out=out_rows[:, i * GROUP : (i + 1) * GROUP, :], in_=z[:])
+
+        for i in range(LEAD):
+            transposes(i)
+            regroup(i)
+            quantise(i)
+        for i in range(GROUPS):
+            ahead = i + LEAD
+            if ahead < GROUPS:
+                transposes(ahead)
+            matmuls(i)
+            if ahead < GROUPS:
+                regroup(ahead)
+            add_bias(i)
+            if ahead < GROUPS:
+                quantise(ahead)
+            gate(i)
+            multiply_and_store(i)

@@ -22,7 +22,6 @@ BLOCKS = PASSES * HALVES
 ROWS_PER_PARTITION = BATCH // P
 GROUP = 2
 GROUPS = ROWS_PER_PARTITION // GROUP
-LEAD = 2
 N_TILES = FEAT // P
 
 FLOPS = 2 * BATCH * (PASSES * FEAT) * FEAT
@@ -38,7 +37,8 @@ def tile_dynamicmemorycell_pa_t_kernel(tc, input_tensor, previous_memory, fg_w, 
     with ExitStack() as ctx:
         consts = ctx.enter_context(tc.tile_pool(name="consts", bufs=1))
         inputs = ctx.enter_context(tc.tile_pool(name="inputs", bufs=GROUPS))
-        stage = ctx.enter_context(tc.tile_pool(name="stage", bufs=LEAD + 2))
+        stage = ctx.enter_context(tc.tile_pool(name="stage", bufs=3))
+        results = ctx.enter_context(tc.tile_pool(name="results", bufs=GROUPS // 2))
         psum_t = ctx.enter_context(tc.psum_pool(name="psum_t", bufs=2 * GROUP))
         psum_acc = ctx.enter_context(tc.psum_pool(name="psum_acc", bufs=2 * GROUP))
         ctx.enter_context(tc.manual_schedule())
@@ -146,7 +146,7 @@ def tile_dynamicmemorycell_pa_t_kernel(tc, input_tensor, previous_memory, fg_w, 
                 acc_of[(i, r)] = acc
 
         def add_bias(i):
-            z = stage.tile([P, GROUP, FEAT], F32)
+            z = results.tile([P, GROUP, FEAT], F32)
             for r in range(GROUP):
                 nc.vector.tensor_tensor(out=z[:, r, :], in0=acc_of[(i, r)][:], in1=bias[:], op=ADD)
             z_of[i] = z
@@ -157,23 +157,26 @@ def tile_dynamicmemorycell_pa_t_kernel(tc, input_tensor, previous_memory, fg_w, 
 
         def multiply_and_store(i):
             z = z_of[i]
-            nc.vector.tensor_tensor(out=z[:, 0, :], in0=z[:, 0, :], in1=m_groups[i][:, 0, :], op=MULT)
-            nc.gpsimd.tensor_tensor(out=z[:, 1, :], in0=z[:, 1, :], in1=m_groups[i][:, 1, :], op=MULT)
-            nc.sync.dma_start(out=out_rows[:, i * GROUP : (i + 1) * GROUP, :], in_=z[:])
+            engines = (nc.vector if i == GROUPS - 1 else nc.gpsimd, nc.vector)
+            for r in range(GROUP):
+                engines[r].tensor_tensor(out=z[:, r, :], in0=z[:, r, :], in1=m_groups[i][:, r, :], op=MULT)
+                nc.sync.dma_start(out=out_rows[:, i * GROUP + r, :], in_=z[:, r, :])
 
-        for i in range(LEAD):
-            transposes(i)
-            regroup(i)
-            quantise(i)
-        for i in range(GROUPS):
-            ahead = i + LEAD
-            if ahead < GROUPS:
-                transposes(ahead)
-            matmuls(i)
-            if ahead < GROUPS:
-                regroup(ahead)
-            add_bias(i)
-            if ahead < GROUPS:
-                quantise(ahead)
-            gate(i)
-            multiply_and_store(i)
+        transposes(0)
+        regroup(0)
+        quantise(0)
+        for i in range(GROUPS + 1):
+            if i + 1 < GROUPS:
+                transposes(i + 1)
+            if i < GROUPS:
+                matmuls(i)
+            if i + 1 < GROUPS:
+                regroup(i + 1)
+            if i >= 1:
+                gate(i - 1)
+            if i + 1 < GROUPS:
+                quantise(i + 1)
+            if i < GROUPS:
+                add_bias(i)
+            if i >= 1:
+                multiply_and_store(i - 1)

@@ -41,7 +41,6 @@ def tile_dynamicmemorycell_pa_t_kernel(tc, input_tensor, previous_memory, fg_w, 
         results = ctx.enter_context(tc.tile_pool(name="results", bufs=GROUPS // 2))
         psum_t = ctx.enter_context(tc.psum_pool(name="psum_t", bufs=2 * GROUP))
         psum_acc = ctx.enter_context(tc.psum_pool(name="psum_acc", bufs=2 * GROUP))
-        ctx.enter_context(tc.manual_schedule())
 
         w_sb = consts.tile([P, N_TILES, PASSES * FEAT], BF16)
         for j in range(N_TILES):

from contextlib import ExitStack

import concourse.mybir as mybir
from concourse.masks import make_identity

F32 = mybir.dt.float32
BF16 = mybir.dt.bfloat16
U32 = mybir.dt.uint32
U8 = mybir.dt.uint8
FP8X4 = mybir.dt.float8_e4m3fn_x4
ADD = mybir.AluOpType.add
MULT = mybir.AluOpType.mult
SIGMOID = mybir.ActivationFunctionType.Sigmoid

P = 128
BATCH = 4096
FEAT = 512
PASSES = 2
PACK = 4
HALVES = 2
BLOCKS = PASSES * HALVES
ROWS_PER_PARTITION = BATCH // P
GROUP = 2
GROUPS = ROWS_PER_PARTITION // GROUP
N_TILES = FEAT // P

FLOPS = 2 * BATCH * (PASSES * FEAT) * FEAT


def tile_dynamicmemorycell_pa_t_kernel(tc, input_tensor, previous_memory, fg_w, fg_b, out):
    nc = tc.nc

    m_rows = previous_memory.rearrange("(p r) k -> p r k", r=ROWS_PER_PARTITION)
    x_rows = input_tensor.rearrange("(p r) k -> p r k", r=ROWS_PER_PARTITION)
    out_rows = out.rearrange("(p r) n -> p r n", r=ROWS_PER_PARTITION)

    with ExitStack() as ctx:
        consts = ctx.enter_context(tc.tile_pool(name="consts", bufs=1))
        inputs = ctx.enter_context(tc.tile_pool(name="inputs", bufs=GROUPS))
        stage = ctx.enter_context(tc.tile_pool(name="stage", bufs=3))
        results = ctx.enter_context(tc.tile_pool(name="results", bufs=GROUPS // 2))
        psum_t = ctx.enter_context(tc.psum_pool(name="psum_t", bufs=2 * GROUP))
        psum_acc = ctx.enter_context(tc.psum_pool(name="psum_acc", bufs=2 * GROUP))

        w_sb = consts.tile([P, N_TILES, PASSES * FEAT], BF16)
        for j in range(N_TILES):
            nc.sync.dma_start(out=w_sb[:, j, :], in_=fg_w[j * P : (j + 1) * P, :])
        bias_row = consts.tile([P, FEAT], BF16)
        nc.vector.memset(bias_row[:], 0.0)
        nc.sync.dma_start(out=bias_row[0:1, :], in_=fg_b.rearrange("(o n) -> o n", o=1))
        m_groups = []
        x_groups = []
        for i in range(GROUPS):
            rows = slice(i * GROUP, (i + 1) * GROUP)
            m_sb = inputs.tile([P, GROUP, FEAT], BF16)
            nc.sync.dma_start(out=m_sb[:], in_=m_rows[:, rows, :])
            x_sb = inputs.tile([P, GROUP, FEAT], BF16)
            nc.sync.dma_start(out=x_sb[:], in_=x_rows[:, rows, :])
            m_groups.append(m_sb)
            x_groups.append(x_sb)

        ident = consts.tile([P, P], F32)
        make_identity(nc, ident[:])
        ones = consts.tile([P, P], BF16)
        nc.vector.memset(ones[:], 1.0)
        warm = consts.tile([P, 1], F32)
        nc.vector.memset(warm[:], 0.0)
        nc.scalar.activation(out=warm[:], in_=warm[:], func=SIGMOID)

        w_words = w_sb[:].bitcast(F32)
        w_grouped = consts.tile([P, PASSES, FEAT, PACK], BF16, align_bytes=64)
        w_grouped_words = w_grouped[:].bitcast(F32)
        for j in range(N_TILES):
            wt = psum_t.tile([P, BLOCKS, P], F32, tag="xt")
            for q in range(BLOCKS):
                nc.tensor.transpose(wt[:, q, :], w_words[:, j, q * P : (q + 1) * P], ident[:])
            nc.vector.tensor_copy(
                out=w_grouped_words[:, :, j * P : (j + 1) * P, :],
                in_=wt[:].rearrange("p (g u) n -> p g n u", u=HALVES),
            )
        w_codes = consts.tile([P, PASSES, FEAT], U32, align_bytes=64)
        w_scales = consts.tile([P, PASSES, FEAT], U8, align_bytes=64)
        for g in range(PASSES):
            nc.vector.quantize_mx(
                out=w_codes[:, g, :].bitcast(FP8X4),
                scales=w_scales[:, g, :],
                in_=w_grouped[:, g, :, :].rearrange("p n t -> p (n t)"),
            )

        bias_sum = psum_acc.tile([P, FEAT], F32, tag="acc")
        nc.tensor.matmul(out=bias_sum[:], lhsT=ones[:], rhs=bias_row[:], start=True, stop=True)
        bias = consts.tile([P, FEAT], F32)
        nc.vector.tensor_copy(out=bias[:], in_=bias_sum[:])

        banks = {}
        grouped_of = {}
        codes_of = {}
        scales_of = {}
        acc_of = {}
        z_of = {}

        def transposes(i):
            for r in range(GROUP):
                xt = psum_t.tile([P, BLOCKS, P], F32, tag="xt")
                for g, src in enumerate((m_groups[i], x_groups[i])):
                    words = src[:].bitcast(F32)
                    for u in range(HALVES):
                        nc.tensor.transpose(xt[:, g * HALVES + u, :], words[:, r, u * P : (u + 1) * P], ident[:])
                banks[(i, r)] = xt

        def regroup(i):
            grouped = stage.tile([P, GROUP, PASSES, P, PACK], BF16, align_bytes=64)
            grouped_words = grouped[:].bitcast(F32)
            for r in range(GROUP):
                nc.scalar.copy(
                    out=grouped_words[:, r, :, :, :],
                    in_=banks[(i, r)][:].rearrange("p (g u) b -> p g b u", u=HALVES),
                )
            grouped_of[i] = grouped

        def quantise(i):
            codes = stage.tile([P, GROUP, PASSES, P], U32, align_bytes=64)
            scales = stage.tile([P, GROUP, PASSES, P], U8, align_bytes=64)
            nc.vector.quantize_mx(
                out=codes[:].rearrange("p r g b -> p (r g b)").bitcast(FP8X4),
                scales=scales[:].rearrange("p r g b -> p (r g b)"),
                in_=grouped_of[i][:].rearrange("p r g b t -> p (r g b t)"),
            )
            codes_of[i] = codes
            scales_of[i] = scales

        def matmuls(i):
            for r in range(GROUP):
                acc = psum_acc.tile([P, FEAT], F32, tag="acc")
                for g in range(PASSES):
                    nc.tensor.matmul_mx(
                        out=acc[:],
                        lhsT=codes_of[i][:, r, g, :].bitcast(FP8X4),
                        lhsT_scale=scales_of[i][:, r, g, :],
                        rhs=w_codes[:, g, :].bitcast(FP8X4),
                        rhs_scale=w_scales[:, g, :],
                        start=(g == 0),
                        stop=(g == PASSES - 1),
                    )
                acc_of[(i, r)] = acc

        def add_bias(i):
            z = results.tile([P, GROUP, FEAT], F32)
            for r in range(GROUP):
                nc.vector.tensor_tensor(out=z[:, r, :], in0=acc_of[(i, r)][:], in1=bias[:], op=ADD)
            z_of[i] = z

        def gate(i):
            for r in range(GROUP):
                nc.scalar.activation(out=z_of[i][:, r, :], in_=z_of[i][:, r, :], func=SIGMOID)

        def multiply_and_store(i):
            z = z_of[i]
            engines = (nc.vector if i == GROUPS - 1 else nc.gpsimd, nc.vector)
            for r in range(GROUP):
                engines[r].tensor_tensor(out=z[:, r, :], in0=z[:, r, :], in1=m_groups[i][:, r, :], op=MULT)
                nc.sync.dma_start(out=out_rows[:, i * GROUP + r, :], in_=z[:, r, :])

        transposes(0)
        regroup(0)
        quantise(0)
        for i in range(GROUPS + 1):
            if i + 1 < GROUPS:
                transposes(i + 1)
            if i < GROUPS:
                matmuls(i)
            if i + 1 < GROUPS:
                regroup(i + 1)
            if i >= 1:
                gate(i - 1)
            if i + 1 < GROUPS:
                quantise(i + 1)
            if i < GROUPS:
                add_bias(i)
            if i >= 1:
                multiply_and_store(i - 1)
